import numpy as np
import ml_dtypes


def mxq(x, axis, fmt="e4m3"):
    dtype, down = {"e4m3": (ml_dtypes.float8_e4m3fn, 7), "e5m2": (ml_dtypes.float8_e5m2, 14)}[fmt]
    v = np.moveaxis(np.asarray(x, np.float32).astype(ml_dtypes.bfloat16).astype(np.float64), axis, -1)
    blocks = v.reshape(v.shape[:-1] + (-1, 32))
    amax = np.abs(blocks).max(-1, keepdims=True)
    byte = np.maximum(np.where(amax > 0, np.frexp(amax)[1] - 1 + 127, 0) - down, 1)
    scale = np.exp2(byte - 127.0)
    codes = (blocks / scale).astype(np.float32).astype(dtype).astype(np.float64)
    return np.moveaxis((codes * scale).reshape(v.shape), -1, axis)


WIDE = False


def mx_kscale(k):
    if not WIDE:
        return np.ones(k)
    levels = np.array([10, -10, 5, -5, 0])
    a = np.random.permutation(np.resize(levels, k // 512 * 4)).reshape(k // 512, 4)
    idx = np.arange(k)
    return np.exp2(a[idx // 512, idx % 128 // 32])


BF16 = ml_dtypes.bfloat16


def bf(x):
    return np.asarray(x, np.float32).astype(BF16)


def f64(x):
    return np.asarray(x).astype(np.float64)


E2M1 = np.array([0.0, 0.5, 1.0, 1.5, 2.0, 3.0, 4.0, 6.0, -0.0, -0.5, -1.0, -1.5, -2.0, -3.0, -4.0, -6.0])


def pack_weight(w, fmt):
    k, n = w.shape
    w = f64(bf(w)).reshape(k // 32, 32, n)
    amax = np.abs(w).max(1)
    if fmt == "e4m3":
        byte = np.frexp(amax)[1] - 1 + 127 - 7
    else:
        mant, ex = np.frexp(amax / 6.0)
        byte = np.where(mant > 0.5, ex, ex - 1) + 127
    byte = np.clip(np.where(amax > 0, byte, 1), 1, 254)
    scaled = (w * np.exp2(127.0 - byte)[:, None, :]).reshape(k, n).astype(np.float32)
    by_word = np.ascontiguousarray(scaled.reshape(k // 512, 128, 4, n).transpose(0, 1, 3, 2))
    if fmt == "e4m3":
        words = by_word.astype(ml_dtypes.float8_e4m3fn).view(np.uint8)
    else:
        c = by_word.astype(ml_dtypes.float4_e2m1fn).view(np.uint8) & 0xF
        words = c[..., 0::2] | (c[..., 1::2] << 4)
    return np.ascontiguousarray(words), np.ascontiguousarray(byte.astype(np.uint8).reshape(k // 512, 16, n))


def unpack_weight(words, scales, fmt):
    g, p, n, _ = words.shape
    if fmt == "e4m3":
        vals = np.ascontiguousarray(words).view(ml_dtypes.float8_e4m3fn).astype(np.float64)
    else:
        nib = np.empty((g, p, n, 4), np.uint8)
        nib[..., 0::2] = words & 0xF
        nib[..., 1::2] = words >> 4
        vals = E2M1[nib]
    vals = vals * np.repeat(np.exp2(scales.astype(np.float64) - 127.0), 8, axis=1)[..., None]
    return vals.transpose(0, 1, 3, 2).reshape(g * 512, n)

def pack4(w):
    words, scales = pack_weight(w, "e2m1")
    return words.reshape(words.shape[0], 128, -1), scales


def unpack4(words, scales):
    return unpack_weight(words.reshape(words.shape[0], 128, -1, 2), scales, "e2m1")


B, C, T, E, H = 1, 48, 128, 512, 4
D = E // H
S = C * T


def heads(y):
    return np.moveaxis(y.reshape(B, C, T, H, D), 3, 1)


def setup_inputs():
    s = mx_kscale(E)
    hidden_states = bf(np.random.standard_normal((B, S, E)) * s)
    wk_words, wk_scales = pack4((np.random.standard_normal((E, E)) * 2.0 / np.sqrt(E) / s[None, :]).T)
    bk = bf(np.random.standard_normal(E) * 0.3)
    wv_words, wv_scales = pack4((np.random.standard_normal((E, E)) * 2.0 / np.sqrt(E) / s[None, :]).T)
    bv = bf(np.random.standard_normal(E) * 0.3)
    return {"hidden_states": hidden_states,
            "wk_words": wk_words,
            "wk_scales": wk_scales,
            "bk": bk,
            "wv_words": wv_words,
            "wv_scales": wv_scales,
            "bv": bv}


def reference(hidden_states, wk_words, wk_scales, bk, wv_words, wv_scales, bv):
    xq = mxq(f64(hidden_states), 2, "e4m3")
    k = heads((xq @ unpack4(wk_words, wk_scales)) + f64(bk))
    v = heads((xq @ unpack4(wv_words, wv_scales)) + f64(bv))
    return k, v, k.mean(axis=3), v.mean(axis=3)

@@ -1,0 +1,227 @@
+from contextlib import ExitStack
+
+import concourse.mybir as mybir
+from concourse.masks import make_identity
+
+F32 = mybir.dt.float32
+BF16 = mybir.dt.bfloat16
+I32 = mybir.dt.int32
+U32 = mybir.dt.uint32
+U8 = mybir.dt.uint8
+FP8X4 = mybir.dt.float8_e4m3fn_x4
+FP4X4 = mybir.dt.float4_e2m1fn_x4
+ADD = mybir.AluOpType.add
+MULT = mybir.AluOpType.mult
+
+P = 128
+TOKENS = 6144
+WIDTH = 512
+HEADS = 4
+HEAD_DIM = 128
+CHUNK = 128
+N_CHUNKS = TOKENS // CHUNK
+
+RUN = 16
+GROUP = P * RUN
+N_GROUPS = TOKENS // GROUP
+PARTS_PER_CHUNK = CHUNK // RUN
+CHUNKS_PER_GROUP = GROUP // CHUNK
+
+BUNCH = 4
+UNIT = 8
+N_BUNCHES = N_GROUPS * RUN // BUNCH
+N_UNITS = N_GROUPS * RUN // UNIT
+UNITS_PER_GROUP = RUN // UNIT
+SCALAR_EVERY = 4
+
+V_ROW = 64
+
+FLOPS = 2 * TOKENS * WIDTH * 2 * WIDTH
+
+
+def tile_chunkedattention_pb_t_kernel(
+    tc, hidden_states, wk_words, wk_scales, bk, wv_words, wv_scales, bv, out_0, out_1, out_2, out_3
+):
+    nc = tc.nc
+    with ExitStack() as ctx:
+        ctx.enter_context(tc.manual_schedule())
+        const = ctx.enter_context(tc.tile_pool(name="const", bufs=1))
+        x_pool = ctx.enter_context(tc.tile_pool(name="x", bufs=N_BUNCHES))
+        grouped_pool = ctx.enter_context(tc.tile_pool(name="grouped", bufs=3))
+        codes_pool = ctx.enter_context(tc.tile_pool(name="codes", bufs=4))
+        out_pool = ctx.enter_context(tc.tile_pool(name="out", bufs=4))
+        sums_pool = ctx.enter_context(tc.tile_pool(name="sums", bufs=2))
+        psum_xt = ctx.enter_context(tc.psum_pool(name="psum_xt", bufs=2))
+        psum_prod = ctx.enter_context(tc.psum_pool(name="psum_prod", bufs=3))
+        psum_acc = ctx.enter_context(tc.psum_pool(name="psum_acc", bufs=1))
+        psum_mean = ctx.enter_context(tc.psum_pool(name="psum_mean", bufs=1))
+
+        x_rows = hidden_states[0].rearrange("(g p j) k -> g p j k", p=P, j=RUN)
+        words_in = (wk_words, wv_words)
+        scales_in = (wk_scales, wv_scales)
+        bias_in = (bk, bv)
+        rows_out = [
+            o[0].rearrange("h c t d -> h (c t) d").rearrange("h (g p j) d -> g p h j d", p=P, j=RUN)
+            for o in (out_0, out_1)
+        ]
+        means_out = [o[0].rearrange("h c d -> c h d") for o in (out_2, out_3)]
+
+        w_words = const.tile([P, 2, 2 * WIDTH], U8, align_bytes=64)
+        w_scales = const.tile([P, 2, WIDTH], U8, align_bytes=64)
+        bias_row = const.tile([P, 2 * WIDTH], BF16)
+        ones = const.tile([P, P], BF16)
+        ident = const.tile([P, P], F32)
+        window = const.tile([P, V_ROW + (N_GROUPS - 1) * CHUNKS_PER_GROUP + P], F32)
+        bias = const.tile([P, 2, WIDTH], F32)
+        mean_sb = const.tile([P, WIDTH], F32)
+
+        nc.vector.memset(w_scales[:].bitcast(I32), 0)
+        nc.vector.memset(bias_row[:].bitcast(I32), 0)
+        nc.vector.memset(ones[:], 1.0)
+        nc.vector.memset(window[:], 0.0)
+        make_identity(nc, ident[:])
+
+        def load_x(b):
+            x_b = x_pool.tile([P, BUNCH, WIDTH], BF16)
+            g, first = divmod(b * BUNCH, RUN)
+            nc.sync.dma_start(out=x_b[:], in_=x_rows[g, :, first : first + BUNCH, :])
+            return x_b
+
+        def load_weight(kv):
+            nc.sync.dma_start(out=w_words[:, kv, :].bitcast(I32), in_=words_in[kv][0].bitcast(I32))
+            for quad in range(4):
+                nc.sync.dma_start(
+                    out=w_scales[32 * quad : 32 * quad + 4, kv, :].bitcast(I32),
+                    in_=scales_in[kv][0, 4 * quad : 4 * quad + 4, :].bitcast(I32),
+                )
+
+        for kv in range(2):
+            nc.scalar.dma_start(
+                out=bias_row[0:1, kv * WIDTH : (kv + 1) * WIDTH], in_=bias_in[kv].unsqueeze(0)
+            )
+        x_tiles = [load_x(0), load_x(1)]
+        load_weight(0)
+        load_weight(1)
+        for b in range(2, N_BUNCHES):
+            x_tiles.append(load_x(b))
+
+        for kv in range(2):
+            spread = psum_prod.tile([P, WIDTH], F32, tag="prod")
+            nc.tensor.matmul(
+                out=spread[:], lhsT=ones[:], rhs=bias_row[:, kv * WIDTH : (kv + 1) * WIDTH], start=True, stop=True
+            )
+            nc.scalar.copy(out=bias[:, kv, :], in_=spread[:])
+
+        last = V_ROW + (N_GROUPS - 1) * CHUNKS_PER_GROUP
+        nc.vector.tensor_reduce(
+            out=window[:, last : last + CHUNKS_PER_GROUP],
+            in_=ident[:].rearrange("p (c i) -> p c i", i=PARTS_PER_CHUNK),
+            axis=mybir.AxisListType.X,
+            op=ADD,
+        )
+
+        grouped_tiles = {}
+        code_tiles = {}
+
+        def transpose_bunch(b):
+            grouped = grouped_pool.tile([P, BUNCH, P, 4], BF16, align_bytes=64)
+            grouped_words = grouped[:].bitcast(F32)
+            for pair in range(BUNCH // 2):
+                xt = psum_xt.tile([P, 2, 2, P], F32)
+                for s in range(2):
+                    x_words = x_tiles[b][:, 2 * pair + s, :].bitcast(F32)
+                    for u in range(2):
+                        nc.tensor.transpose(xt[:, s, u, :], x_words[:, u : WIDTH // 2 : 2], ident[:])
+                nc.scalar.copy(
+                    out=grouped_words[:, 2 * pair : 2 * pair + 2, :, :],
+                    in_=xt[:].rearrange("p s u t -> p s t u"),
+                )
+            grouped_tiles[b] = grouped
+
+        def quantise_bunch(b):
+            codes = codes_pool.tile([P, BUNCH * P], U32, align_bytes=64)
+            planes = codes_pool.tile([P, BUNCH * P], U8, align_bytes=64)
+            nc.vector.quantize_mx(
+                out=codes[:].bitcast(FP8X4),
+                scales=planes[:],
+                in_=grouped_tiles[b][:].rearrange("p s t f -> p (s t f)"),
+            )
+            code_tiles[b] = (codes, planes)
+
+        def project(target, slot, kv, start, stop):
+            codes, planes = code_tiles[slot // BUNCH]
+            cols = slice((slot % BUNCH) * P, (slot % BUNCH + 1) * P)
+            nc.tensor.matmul_mx(
+                out=target[:],
+                lhsT=codes[:, cols].bitcast(FP8X4),
+                lhsT_scale=planes[:, cols],
+                rhs=w_words[:, kv, :].bitcast(FP4X4),
+                rhs_scale=w_scales[:, kv, :],
+                start=start,
+                stop=stop,
+            )
+
+        mean_ps = psum_mean.tile([P, WIDTH], F32)
+        acc_tiles = {}
+        sums_tiles = {}
+
+        def add_group_to_means(g, kv):
+            row = kv * V_ROW + g * CHUNKS_PER_GROUP
+            nc.tensor.matmul(
+                out=mean_ps[:],
+                lhsT=window[:, last - row : last - row + P],
+                rhs=sums_tiles[(g, kv)][:],
+                start=(g == 0 and kv == 0),
+                stop=(g == N_GROUPS - 1 and kv == 1),
+            )
+
+        transpose_bunch(0)
+        transpose_bunch(1)
+        quantise_bunch(0)
+
+        closed = None
+        for phase in range(2 * N_UNITS):
+            unit, kv = divmod(phase, 2)
+            g, unit_in_group = divmod(unit, UNITS_PER_GROUP)
+            bias_kv = bias[:, kv, :].rearrange("p (h d) -> p h d", h=HEADS)
+            if phase + 1 < N_BUNCHES:
+                quantise_bunch(phase + 1)
+            if unit_in_group == 0:
+                acc = psum_acc.tile([P, WIDTH], F32, tag="acc%d" % kv)
+                acc_tiles[kv] = acc
+            rows = out_pool.tile([P, HEADS, UNIT, HEAD_DIM], F32)
+            for i in range(UNIT):
+                slot = unit * UNIT + i
+                in_group = slot % RUN
+                if i == UNIT // 2:
+                    if phase + 2 < N_BUNCHES:
+                        transpose_bunch(phase + 2)
+                    if closed is not None:
+                        add_group_to_means(closed[0], closed[1])
+                        closed = None
+                project(acc_tiles[kv], slot, kv, start=(in_group == 0), stop=(in_group == RUN - 1))
+                prod = psum_prod.tile([P, WIDTH], F32, tag="prod")
+                project(prod, slot, kv, start=True, stop=True)
+                prod_heads = prod[:].rearrange("p (h d) -> p h d", h=HEADS)
+                if i % SCALAR_EVERY == SCALAR_EVERY - 1:
+                    nc.scalar.copy(out=rows[:, :, i, :], in_=prod_heads)
+                    nc.gpsimd.tensor_tensor(out=rows[:, :, i, :], in0=rows[:, :, i, :], in1=bias_kv, op=ADD)
+                else:
+                    nc.vector.tensor_tensor(out=rows[:, :, i, :], in0=prod_heads, in1=bias_kv, op=ADD)
+            if unit_in_group == UNITS_PER_GROUP - 1:
+                sums = sums_pool.tile([P, WIDTH], F32)
+                nc.vector.scalar_tensor_tensor(
+                    out=sums[:], in0=bias[:, kv, :], scalar=float(RUN), in1=acc_tiles[kv][:], op0=MULT, op1=ADD
+                )
+                sums_tiles[(g, kv)] = sums
+                closed = (g, kv)
+            first = unit_in_group * UNIT
+            nc.sync.dma_start(out=rows_out[kv][g, :, :, first : first + UNIT, :], in_=rows[:])
+
+        add_group_to_means(closed[0], closed[1])
+        nc.scalar.mul(out=mean_sb[:], in_=mean_ps[:], mul=1.0 / CHUNK)
+        for kv in range(2):
+            nc.sync.dma_start(
+                out=means_out[kv],
+                in_=mean_sb[kv * V_ROW : kv * V_ROW + N_CHUNKS, :].rearrange("c (h d) -> c h d", h=HEADS),
+            )

@@ -33,6 +33,7 @@ N_BUNCHES = N_GROUPS * RUN // BUNCH
 N_UNITS = N_GROUPS * RUN // UNIT
 UNITS_PER_GROUP = RUN // UNIT
 SCALAR_EVERY = 4
+TAIL_SLOTS = 2
 
 V_ROW = 64
 
@@ -47,9 +48,10 @@ def tile_chunkedattention_pb_t_kernel(
         ctx.enter_context(tc.manual_schedule())
         const = ctx.enter_context(tc.tile_pool(name="const", bufs=1))
         x_pool = ctx.enter_context(tc.tile_pool(name="x", bufs=N_BUNCHES))
+        sorted_pool = ctx.enter_context(tc.tile_pool(name="sorted", bufs=3))
         grouped_pool = ctx.enter_context(tc.tile_pool(name="grouped", bufs=3))
         codes_pool = ctx.enter_context(tc.tile_pool(name="codes", bufs=4))
-        out_pool = ctx.enter_context(tc.tile_pool(name="out", bufs=4))
+        out_pool = ctx.enter_context(tc.tile_pool(name="out", bufs=5))
         sums_pool = ctx.enter_context(tc.tile_pool(name="sums", bufs=2))
         psum_xt = ctx.enter_context(tc.psum_pool(name="psum_xt", bufs=2))
         psum_prod = ctx.enter_context(tc.psum_pool(name="psum_prod", bufs=3))
@@ -120,8 +122,19 @@ def tile_chunkedattention_pb_t_kernel(
             op=ADD,
         )
 
+        sorted_tiles = {}
         grouped_tiles = {}
         code_tiles = {}
+
+        def sort_bunch(b):
+            x_sorted = sorted_pool.tile([P, BUNCH, 2, P], F32)
+            for pair in range(BUNCH // 2):
+                two = slice(2 * pair, 2 * pair + 2)
+                nc.scalar.copy(
+                    out=x_sorted[:, two, :, :],
+                    in_=x_tiles[b][:, two, :].bitcast(F32).rearrange("p s (w u) -> p s u w", u=2),
+                )
+            sorted_tiles[b] = x_sorted
 
         def transpose_bunch(b):
             grouped = grouped_pool.tile([P, BUNCH, P, 4], BF16, align_bytes=64)
@@ -129,9 +142,8 @@ def tile_chunkedattention_pb_t_kernel(
             for pair in range(BUNCH // 2):
                 xt = psum_xt.tile([P, 2, 2, P], F32)
                 for s in range(2):
-                    x_words = x_tiles[b][:, 2 * pair + s, :].bitcast(F32)
                     for u in range(2):
-                        nc.tensor.transpose(xt[:, s, u, :], x_words[:, u : WIDTH // 2 : 2], ident[:])
+                        nc.tensor.transpose(xt[:, s, u, :], sorted_tiles[b][:, 2 * pair + s, u, :], ident[:])
                 nc.scalar.copy(
                     out=grouped_words[:, 2 * pair : 2 * pair + 2, :, :],
                     in_=xt[:].rearrange("p s u t -> p s t u"),
@@ -175,8 +187,11 @@ def tile_chunkedattention_pb_t_kernel(
                 stop=(g == N_GROUPS - 1 and kv == 1),
             )
 
+        sort_bunch(0)
         transpose_bunch(0)
+        sort_bunch(1)
         transpose_bunch(1)
+        sort_bunch(2)
         quantise_bunch(0)
 
         closed = None
@@ -190,12 +205,15 @@ def tile_chunkedattention_pb_t_kernel(
                 acc = psum_acc.tile([P, WIDTH], F32, tag="acc%d" % kv)
                 acc_tiles[kv] = acc
             rows = out_pool.tile([P, HEADS, UNIT, HEAD_DIM], F32)
+            store_slots = TAIL_SLOTS if phase == 2 * N_UNITS - 1 else UNIT
             for i in range(UNIT):
                 slot = unit * UNIT + i
                 in_group = slot % RUN
                 if i == UNIT // 2:
                     if phase + 2 < N_BUNCHES:
                         transpose_bunch(phase + 2)
+                    if phase + 3 < N_BUNCHES:
+                        sort_bunch(phase + 3)
                     if closed is not None:
                         add_group_to_means(closed[0], closed[1])
                         closed = None
@@ -203,11 +221,15 @@ def tile_chunkedattention_pb_t_kernel(
                 prod = psum_prod.tile([P, WIDTH], F32, tag="prod")
                 project(prod, slot, kv, start=True, stop=True)
                 prod_heads = prod[:].rearrange("p (h d) -> p h d", h=HEADS)
-                if i % SCALAR_EVERY == SCALAR_EVERY - 1:
+                if i % SCALAR_EVERY == 1:
                     nc.scalar.copy(out=rows[:, :, i, :], in_=prod_heads)
                     nc.gpsimd.tensor_tensor(out=rows[:, :, i, :], in0=rows[:, :, i, :], in1=bias_kv, op=ADD)
                 else:
                     nc.vector.tensor_tensor(out=rows[:, :, i, :], in0=prod_heads, in1=bias_kv, op=ADD)
+                if (i + 1) % store_slots == 0:
+                    done = slice(i + 1 - store_slots, i + 1)
+                    in_run = slice(in_group + 1 - store_slots, in_group + 1)
+                    nc.sync.dma_start(out=rows_out[kv][g, :, :, in_run, :], in_=rows[:, :, done, :])
             if unit_in_group == UNITS_PER_GROUP - 1:
                 sums = sums_pool.tile([P, WIDTH], F32)
                 nc.vector.scalar_tensor_tensor(
@@ -215,8 +237,6 @@ def tile_chunkedattention_pb_t_kernel(
                 )
                 sums_tiles[(g, kv)] = sums
                 closed = (g, kv)
-            first = unit_in_group * UNIT
-            nc.sync.dma_start(out=rows_out[kv][g, :, :, first : first + UNIT, :], in_=rows[:])
 
         add_group_to_means(closed[0], closed[1])
         nc.scalar.mul(out=mean_sb[:], in_=mean_ps[:], mul=1.0 / CHUNK)

@@ -20,6 +20,7 @@ HEADS = 4
 HEAD_DIM = 128
 CHUNK = 128
 N_CHUNKS = TOKENS // CHUNK
+MEAN_ROWS = HEADS * N_CHUNKS
 
 RUN = 16
 GROUP = P * RUN
@@ -32,10 +33,9 @@ UNIT = 8
 N_BUNCHES = N_GROUPS * RUN // BUNCH
 N_UNITS = N_GROUPS * RUN // UNIT
 UNITS_PER_GROUP = RUN // UNIT
+N_PHASES = 2 * N_UNITS
 SCALAR_EVERY = 4
 TAIL_SLOTS = 2
-
-V_ROW = 64
 
 FLOPS = 2 * TOKENS * WIDTH * 2 * WIDTH
 
@@ -56,7 +56,7 @@ def tile_chunkedattention_pb_t_kernel(
         psum_xt = ctx.enter_context(tc.psum_pool(name="psum_xt", bufs=2))
         psum_prod = ctx.enter_context(tc.psum_pool(name="psum_prod", bufs=3))
         psum_acc = ctx.enter_context(tc.psum_pool(name="psum_acc", bufs=1))
-        psum_mean = ctx.enter_context(tc.psum_pool(name="psum_mean", bufs=1))
+        psum_flip = ctx.enter_context(tc.psum_pool(name="psum_flip", bufs=1))
 
         x_rows = hidden_states[0].rearrange("(g p j) k -> g p j k", p=P, j=RUN)
         words_in = (wk_words, wv_words)
@@ -66,21 +66,20 @@ def tile_chunkedattention_pb_t_kernel(
             o[0].rearrange("h c t d -> h (c t) d").rearrange("h (g p j) d -> g p h j d", p=P, j=RUN)
             for o in (out_0, out_1)
         ]
-        means_out = [o[0].rearrange("h c d -> c h d") for o in (out_2, out_3)]
+        means_out = [o[0].rearrange("h c d -> (h c) d") for o in (out_2, out_3)]
 
         w_words = const.tile([P, 2, 2 * WIDTH], U8, align_bytes=64)
         w_scales = const.tile([P, 2, WIDTH], U8, align_bytes=64)
         bias_row = const.tile([P, 2 * WIDTH], BF16)
         ones = const.tile([P, P], BF16)
         ident = const.tile([P, P], F32)
-        window = const.tile([P, V_ROW + (N_GROUPS - 1) * CHUNKS_PER_GROUP + P], F32)
         bias = const.tile([P, 2, WIDTH], F32)
-        mean_sb = const.tile([P, WIDTH], F32)
+        means_t = const.tile([P, 2, HEADS, N_CHUNKS], F32)
+        mean_rows = const.tile([P, 2 * MEAN_ROWS // P, HEAD_DIM], F32)
 
-        nc.vector.memset(w_scales[:].bitcast(I32), 0)
         nc.vector.memset(bias_row[:].bitcast(I32), 0)
+        nc.vector.memset(w_scales[:].bitcast(I32), 0)
         nc.vector.memset(ones[:], 1.0)
-        nc.vector.memset(window[:], 0.0)
         make_identity(nc, ident[:])
 
         def load_x(b):
@@ -101,30 +100,25 @@ def tile_chunkedattention_pb_t_kernel(
             nc.scalar.dma_start(
                 out=bias_row[0:1, kv * WIDTH : (kv + 1) * WIDTH], in_=bias_in[kv].unsqueeze(0)
             )
-        x_tiles = [load_x(0), load_x(1)]
+        x_tiles = [load_x(0), load_x(1), load_x(2)]
         load_weight(0)
         load_weight(1)
-        for b in range(2, N_BUNCHES):
+        for b in range(3, N_BUNCHES):
             x_tiles.append(load_x(b))
-
-        for kv in range(2):
-            spread = psum_prod.tile([P, WIDTH], F32, tag="prod")
-            nc.tensor.matmul(
-                out=spread[:], lhsT=ones[:], rhs=bias_row[:, kv * WIDTH : (kv + 1) * WIDTH], start=True, stop=True
-            )
-            nc.scalar.copy(out=bias[:, kv, :], in_=spread[:])
-
-        last = V_ROW + (N_GROUPS - 1) * CHUNKS_PER_GROUP
-        nc.vector.tensor_reduce(
-            out=window[:, last : last + CHUNKS_PER_GROUP],
-            in_=ident[:].rearrange("p (c i) -> p c i", i=PARTS_PER_CHUNK),
-            axis=mybir.AxisListType.X,
-            op=ADD,
-        )
 
         sorted_tiles = {}
         grouped_tiles = {}
         code_tiles = {}
+        acc_tiles = {}
+        sums_tiles = {}
+
+        def spread_biases():
+            for kv in range(2):
+                spread = psum_prod.tile([P, WIDTH], F32, tag="prod")
+                nc.tensor.matmul(
+                    out=spread[:], lhsT=ones[:], rhs=bias_row[:, kv * WIDTH : (kv + 1) * WIDTH], start=True, stop=True
+                )
+                nc.vector.tensor_copy(out=bias[:, kv, :], in_=spread[:])
 
         def sort_bunch(b):
             x_sorted = sorted_pool.tile([P, BUNCH, 2, P], F32)
@@ -173,59 +167,59 @@ def tile_chunkedattention_pb_t_kernel(
                 stop=stop,
             )
 
-        mean_ps = psum_mean.tile([P, WIDTH], F32)
-        acc_tiles = {}
-        sums_tiles = {}
-
-        def add_group_to_means(g, kv):
-            row = kv * V_ROW + g * CHUNKS_PER_GROUP
-            nc.tensor.matmul(
-                out=mean_ps[:],
-                lhsT=window[:, last - row : last - row + P],
-                rhs=sums_tiles[(g, kv)][:],
-                start=(g == 0 and kv == 0),
-                stop=(g == N_GROUPS - 1 and kv == 1),
+        def add_partitions(g, kv):
+            flipped = psum_flip.tile([P, HEADS, P], F32, tag="flip")
+            for h in range(HEADS):
+                nc.tensor.transpose(
+                    flipped[:, h, :], sums_tiles[(g, kv)][:, h * HEAD_DIM : (h + 1) * HEAD_DIM], ident[:]
+                )
+            nc.vector.tensor_reduce(
+                out=means_t[:, kv, :, g * CHUNKS_PER_GROUP : (g + 1) * CHUNKS_PER_GROUP],
+                in_=flipped[:].rearrange("d h (c i) -> d h c i", i=PARTS_PER_CHUNK),
+                axis=mybir.AxisListType.X,
+                op=ADD,
             )
 
         sort_bunch(0)
-        transpose_bunch(0)
         sort_bunch(1)
-        transpose_bunch(1)
+        transpose_bunch(0)
+        spread_biases()
         sort_bunch(2)
+        transpose_bunch(1)
         quantise_bunch(0)
 
         closed = None
-        for phase in range(2 * N_UNITS):
+        for phase in range(N_PHASES):
             unit, kv = divmod(phase, 2)
             g, unit_in_group = divmod(unit, UNITS_PER_GROUP)
             bias_kv = bias[:, kv, :].rearrange("p (h d) -> p h d", h=HEADS)
+            store_slots = TAIL_SLOTS if phase == N_PHASES - 1 else UNIT
             if phase + 1 < N_BUNCHES:
                 quantise_bunch(phase + 1)
             if unit_in_group == 0:
                 acc = psum_acc.tile([P, WIDTH], F32, tag="acc%d" % kv)
                 acc_tiles[kv] = acc
             rows = out_pool.tile([P, HEADS, UNIT, HEAD_DIM], F32)
-            store_slots = TAIL_SLOTS if phase == 2 * N_UNITS - 1 else UNIT
             for i in range(UNIT):
                 slot = unit * UNIT + i
                 in_group = slot % RUN
                 if i == UNIT // 2:
                     if phase + 2 < N_BUNCHES:
                         transpose_bunch(phase + 2)
-                    if phase + 3 < N_BUNCHES:
-                        sort_bunch(phase + 3)
                     if closed is not None:
-                        add_group_to_means(closed[0], closed[1])
+                        add_partitions(closed[0], closed[1])
                         closed = None
                 project(acc_tiles[kv], slot, kv, start=(in_group == 0), stop=(in_group == RUN - 1))
                 prod = psum_prod.tile([P, WIDTH], F32, tag="prod")
                 project(prod, slot, kv, start=True, stop=True)
                 prod_heads = prod[:].rearrange("p (h d) -> p h d", h=HEADS)
-                if i % SCALAR_EVERY == 1:
+                if i % SCALAR_EVERY == 0:
                     nc.scalar.copy(out=rows[:, :, i, :], in_=prod_heads)
                     nc.gpsimd.tensor_tensor(out=rows[:, :, i, :], in0=rows[:, :, i, :], in1=bias_kv, op=ADD)
                 else:
                     nc.vector.tensor_tensor(out=rows[:, :, i, :], in0=prod_heads, in1=bias_kv, op=ADD)
+                if i == 0 and phase + 3 < N_BUNCHES:
+                    sort_bunch(phase + 3)
                 if (i + 1) % store_slots == 0:
                     done = slice(i + 1 - store_slots, i + 1)
                     in_run = slice(in_group + 1 - store_slots, in_group + 1)
@@ -238,10 +232,19 @@ def tile_chunkedattention_pb_t_kernel(
                 sums_tiles[(g, kv)] = sums
                 closed = (g, kv)
 
-        add_group_to_means(closed[0], closed[1])
-        nc.scalar.mul(out=mean_sb[:], in_=mean_ps[:], mul=1.0 / CHUNK)
+        add_partitions(closed[0], closed[1])
+        means_t_cols = means_t[:].rearrange("d a h c -> d (a h c)")
+        n_blocks = 2 * MEAN_ROWS // P
+        flipped_back = psum_flip.tile([P, n_blocks, HEAD_DIM], F32, tag="flip")
+        for r in range(n_blocks):
+            nc.tensor.transpose(flipped_back[:, r, :], means_t_cols[:, r * P : (r + 1) * P], ident[:])
+        nc.scalar.mul(out=mean_rows[:], in_=flipped_back[:], mul=1.0 / CHUNK)
         for kv in range(2):
-            nc.sync.dma_start(
-                out=means_out[kv],
-                in_=mean_sb[kv * V_ROW : kv * V_ROW + N_CHUNKS, :].rearrange("c (h d) -> c h d", h=HEADS),
-            )
+            for r in range(n_blocks):
+                low = max(kv * MEAN_ROWS, r * P)
+                high = min((kv + 1) * MEAN_ROWS, (r + 1) * P)
+                if low < high:
+                    nc.sync.dma_start(
+                        out=means_out[kv][low - kv * MEAN_ROWS : high - kv * MEAN_ROWS, :],
+                        in_=mean_rows[low - r * P : high - r * P, r, :],
+                    )

@@ -11,7 +11,6 @@ U8 = mybir.dt.uint8
 FP8X4 = mybir.dt.float8_e4m3fn_x4
 FP4X4 = mybir.dt.float4_e2m1fn_x4
 ADD = mybir.AluOpType.add
-MULT = mybir.AluOpType.mult
 
 P = 128
 TOKENS = 6144
@@ -35,6 +34,8 @@ N_UNITS = N_GROUPS * RUN // UNIT
 UNITS_PER_GROUP = RUN // UNIT
 N_PHASES = 2 * N_UNITS
 SCALAR_EVERY = 4
+GPSIMD_SLOT = 2
+N_PSUM_SLOTS = RUN - UNITS_PER_GROUP
 TAIL_SLOTS = 2
 
 FLOPS = 2 * TOKENS * WIDTH * 2 * WIDTH
@@ -53,10 +54,9 @@ def tile_chunkedattention_pb_t_kernel(
         codes_pool = ctx.enter_context(tc.tile_pool(name="codes", bufs=4))
         out_pool = ctx.enter_context(tc.tile_pool(name="out", bufs=5))
         sums_pool = ctx.enter_context(tc.tile_pool(name="sums", bufs=2))
-        psum_xt = ctx.enter_context(tc.psum_pool(name="psum_xt", bufs=2))
-        psum_prod = ctx.enter_context(tc.psum_pool(name="psum_prod", bufs=3))
+        extra_pool = ctx.enter_context(tc.tile_pool(name="extra", bufs=2))
+        psum_prod = ctx.enter_context(tc.psum_pool(name="psum_prod", bufs=6))
         psum_acc = ctx.enter_context(tc.psum_pool(name="psum_acc", bufs=1))
-        psum_flip = ctx.enter_context(tc.psum_pool(name="psum_flip", bufs=1))
 
         x_rows = hidden_states[0].rearrange("(g p j) k -> g p j k", p=P, j=RUN)
         words_in = (wk_words, wv_words)
@@ -74,6 +74,7 @@ def tile_chunkedattention_pb_t_kernel(
         ones = const.tile([P, P], BF16)
         ident = const.tile([P, P], F32)
         bias = const.tile([P, 2, WIDTH], F32)
+        bias_psum_slots = const.tile([P, 2, WIDTH], F32)
         means_t = const.tile([P, 2, HEADS, N_CHUNKS], F32)
         mean_rows = const.tile([P, 2 * MEAN_ROWS // P, HEAD_DIM], F32)
 
@@ -96,11 +97,13 @@ def tile_chunkedattention_pb_t_kernel(
                     in_=scales_in[kv][0, 4 * quad : 4 * quad + 4, :].bitcast(I32),
                 )
 
+        x_tiles = [load_x(0)]
         for kv in range(2):
-            nc.scalar.dma_start(
+            nc.sync.dma_start(
                 out=bias_row[0:1, kv * WIDTH : (kv + 1) * WIDTH], in_=bias_in[kv].unsqueeze(0)
             )
-        x_tiles = [load_x(0), load_x(1), load_x(2)]
+        x_tiles.append(load_x(1))
+        x_tiles.append(load_x(2))
         load_weight(0)
         load_weight(1)
         for b in range(3, N_BUNCHES):
@@ -111,6 +114,7 @@ def tile_chunkedattention_pb_t_kernel(
         code_tiles = {}
         acc_tiles = {}
         sums_tiles = {}
+        extra_tiles = {}
 
         def spread_biases():
             for kv in range(2):
@@ -119,6 +123,7 @@ def tile_chunkedattention_pb_t_kernel(
                     out=spread[:], lhsT=ones[:], rhs=bias_row[:, kv * WIDTH : (kv + 1) * WIDTH], start=True, stop=True
                 )
                 nc.vector.tensor_copy(out=bias[:, kv, :], in_=spread[:])
+                nc.vector.tensor_scalar_mul(out=bias_psum_slots[:, kv, :], in0=bias[:, kv, :], scalar1=float(N_PSUM_SLOTS))
 
         def sort_bunch(b):
             x_sorted = sorted_pool.tile([P, BUNCH, 2, P], F32)
@@ -134,7 +139,7 @@ def tile_chunkedattention_pb_t_kernel(
             grouped = grouped_pool.tile([P, BUNCH, P, 4], BF16, align_bytes=64)
             grouped_words = grouped[:].bitcast(F32)
             for pair in range(BUNCH // 2):
-                xt = psum_xt.tile([P, 2, 2, P], F32)
+                xt = psum_prod.tile([P, 2, 2, P], F32, tag="prod")
                 for s in range(2):
                     for u in range(2):
                         nc.tensor.transpose(xt[:, s, u, :], sorted_tiles[b][:, 2 * pair + s, u, :], ident[:])
@@ -168,7 +173,7 @@ def tile_chunkedattention_pb_t_kernel(
             )
 
         def add_partitions(g, kv):
-            flipped = psum_flip.tile([P, HEADS, P], F32, tag="flip")
+            flipped = psum_prod.tile([P, HEADS, P], F32, tag="prod")
             for h in range(HEADS):
                 nc.tensor.transpose(
                     flipped[:, h, :], sums_tiles[(g, kv)][:, h * HEAD_DIM : (h + 1) * HEAD_DIM], ident[:]
@@ -180,10 +185,10 @@ def tile_chunkedattention_pb_t_kernel(
                 op=ADD,
             )
 
+        spread_biases()
         sort_bunch(0)
         sort_bunch(1)
         transpose_bunch(0)
-        spread_biases()
         sort_bunch(2)
         transpose_bunch(1)
         quantise_bunch(0)
@@ -209,7 +214,8 @@ def tile_chunkedattention_pb_t_kernel(
                     if closed is not None:
                         add_partitions(closed[0], closed[1])
                         closed = None
-                project(acc_tiles[kv], slot, kv, start=(in_group == 0), stop=(in_group == RUN - 1))
+                if i != GPSIMD_SLOT:
+                    project(acc_tiles[kv], slot, kv, start=(in_group == 0), stop=(in_group == RUN - 1))
                 prod = psum_prod.tile([P, WIDTH], F32, tag="prod")
                 project(prod, slot, kv, start=True, stop=True)
                 prod_heads = prod[:].rearrange("p (h d) -> p h d", h=HEADS)
@@ -218,6 +224,14 @@ def tile_chunkedattention_pb_t_kernel(
                     nc.gpsimd.tensor_tensor(out=rows[:, :, i, :], in0=rows[:, :, i, :], in1=bias_kv, op=ADD)
                 else:
                     nc.vector.tensor_tensor(out=rows[:, :, i, :], in0=prod_heads, in1=bias_kv, op=ADD)
+                if i == GPSIMD_SLOT:
+                    if unit_in_group == 0:
+                        extra = extra_pool.tile([P, HEADS, HEAD_DIM], F32, tag="extra%d" % kv)
+                        extra_tiles[kv] = extra
+                        so_far = bias_psum_slots[:, kv, :].rearrange("p (h d) -> p h d", h=HEADS)
+                    else:
+                        so_far = extra_tiles[kv][:]
+                    nc.gpsimd.tensor_tensor(out=extra_tiles[kv][:], in0=rows[:, :, i, :], in1=so_far, op=ADD)
                 if i == 0 and phase + 3 < N_BUNCHES:
                     sort_bunch(phase + 3)
                 if (i + 1) % store_slots == 0:
@@ -226,8 +240,8 @@ def tile_chunkedattention_pb_t_kernel(
                     nc.sync.dma_start(out=rows_out[kv][g, :, :, in_run, :], in_=rows[:, :, done, :])
             if unit_in_group == UNITS_PER_GROUP - 1:
                 sums = sums_pool.tile([P, WIDTH], F32)
-                nc.vector.scalar_tensor_tensor(
-                    out=sums[:], in0=bias[:, kv, :], scalar=float(RUN), in1=acc_tiles[kv][:], op0=MULT, op1=ADD
+                nc.vector.tensor_tensor(
+                    out=sums[:], in0=acc_tiles[kv][:], in1=extra_tiles[kv][:].rearrange("p h d -> p (h d)"), op=ADD
                 )
                 sums_tiles[(g, kv)] = sums
                 closed = (g, kv)
@@ -235,7 +249,7 @@ def tile_chunkedattention_pb_t_kernel(
         add_partitions(closed[0], closed[1])
         means_t_cols = means_t[:].rearrange("d a h c -> d (a h c)")
         n_blocks = 2 * MEAN_ROWS // P
-        flipped_back = psum_flip.tile([P, n_blocks, HEAD_DIM], F32, tag="flip")
+        flipped_back = psum_prod.tile([P, n_blocks, HEAD_DIM], F32, tag="prod")
         for r in range(n_blocks):
             nc.tensor.transpose(flipped_back[:, r, :], means_t_cols[:, r * P : (r + 1) * P], ident[:])
         nc.scalar.mul(out=mean_rows[:], in_=flipped_back[:], mul=1.0 / CHUNK)

@@ -97,14 +97,15 @@ def tile_chunkedattention_pb_t_kernel(
                     in_=scales_in[kv][0, 4 * quad : 4 * quad + 4, :].bitcast(I32),
                 )
 
+        def load_bias(kv):
+            nc.sync.dma_start(out=bias_row[0:1, kv * WIDTH : (kv + 1) * WIDTH], in_=bias_in[kv].unsqueeze(0))
+
         x_tiles = [load_x(0)]
-        for kv in range(2):
-            nc.sync.dma_start(
-                out=bias_row[0:1, kv * WIDTH : (kv + 1) * WIDTH], in_=bias_in[kv].unsqueeze(0)
-            )
-        x_tiles.append(load_x(1))
-        x_tiles.append(load_x(2))
         load_weight(0)
+        x_tiles.append(load_x(1))
+        load_bias(0)
+        x_tiles.append(load_x(2))
+        load_bias(1)
         load_weight(1)
         for b in range(3, N_BUNCHES):
             x_tiles.append(load_x(b))
@@ -116,14 +117,13 @@ def tile_chunkedattention_pb_t_kernel(
         sums_tiles = {}
         extra_tiles = {}
 
-        def spread_biases():
-            for kv in range(2):
-                spread = psum_prod.tile([P, WIDTH], F32, tag="prod")
-                nc.tensor.matmul(
-                    out=spread[:], lhsT=ones[:], rhs=bias_row[:, kv * WIDTH : (kv + 1) * WIDTH], start=True, stop=True
-                )
-                nc.vector.tensor_copy(out=bias[:, kv, :], in_=spread[:])
-                nc.vector.tensor_scalar_mul(out=bias_psum_slots[:, kv, :], in0=bias[:, kv, :], scalar1=float(N_PSUM_SLOTS))
+        def spread_bias(kv):
+            spread = psum_prod.tile([P, WIDTH], F32, tag="prod")
+            nc.tensor.matmul(
+                out=spread[:], lhsT=ones[:], rhs=bias_row[:, kv * WIDTH : (kv + 1) * WIDTH], start=True, stop=True
+            )
+            nc.vector.tensor_copy(out=bias[:, kv, :], in_=spread[:])
+            nc.vector.tensor_scalar_mul(out=bias_psum_slots[:, kv, :], in0=bias[:, kv, :], scalar1=float(N_PSUM_SLOTS))
 
         def sort_bunch(b):
             x_sorted = sorted_pool.tile([P, BUNCH, 2, P], F32)
@@ -135,28 +135,35 @@ def tile_chunkedattention_pb_t_kernel(
                 )
             sorted_tiles[b] = x_sorted
 
-        def transpose_bunch(b):
+        def transpose_bunch(b, direct=False):
             grouped = grouped_pool.tile([P, BUNCH, P, 4], BF16, align_bytes=64)
             grouped_words = grouped[:].bitcast(F32)
             for pair in range(BUNCH // 2):
                 xt = psum_prod.tile([P, 2, 2, P], F32, tag="prod")
                 for s in range(2):
                     for u in range(2):
-                        nc.tensor.transpose(xt[:, s, u, :], sorted_tiles[b][:, 2 * pair + s, u, :], ident[:])
+                        if direct:
+                            words = x_tiles[b][:, 2 * pair + s, :].bitcast(F32)
+                            nc.tensor.transpose(xt[:, s, u, :], words[:, u : WIDTH // 2 : 2], ident[:])
+                        else:
+                            nc.tensor.transpose(xt[:, s, u, :], sorted_tiles[b][:, 2 * pair + s, u, :], ident[:])
                 nc.scalar.copy(
                     out=grouped_words[:, 2 * pair : 2 * pair + 2, :, :],
                     in_=xt[:].rearrange("p s u t -> p s t u"),
                 )
             grouped_tiles[b] = grouped
 
-        def quantise_bunch(b):
+        def quantise_bunch(b, pieces=1):
             codes = codes_pool.tile([P, BUNCH * P], U32, align_bytes=64)
             planes = codes_pool.tile([P, BUNCH * P], U8, align_bytes=64)
-            nc.vector.quantize_mx(
-                out=codes[:].bitcast(FP8X4),
-                scales=planes[:],
-                in_=grouped_tiles[b][:].rearrange("p s t f -> p (s t f)"),
-            )
+            n = BUNCH // pieces
+            for s in range(0, BUNCH, n):
+                cols = slice(s * P, (s + n) * P)
+                nc.vector.quantize_mx(
+                    out=codes[:, cols].bitcast(FP8X4),
+                    scales=planes[:, cols],
+                    in_=grouped_tiles[b][:, s : s + n, :, :].rearrange("p s t f -> p (s t f)"),
+                )
             code_tiles[b] = (codes, planes)
 
         def project(target, slot, kv, start, stop):
@@ -185,13 +192,11 @@ def tile_chunkedattention_pb_t_kernel(
                 op=ADD,
             )
 
-        spread_biases()
-        sort_bunch(0)
-        sort_bunch(1)
-        transpose_bunch(0)
+        transpose_bunch(0, direct=True)
+        quantise_bunch(0, pieces=2)
+        transpose_bunch(1, direct=True)
+        spread_bias(0)
         sort_bunch(2)
-        transpose_bunch(1)
-        quantise_bunch(0)
 
         closed = None
         for phase in range(N_PHASES):
@@ -211,6 +216,8 @@ def tile_chunkedattention_pb_t_kernel(
                 if i == UNIT // 2:
                     if phase + 2 < N_BUNCHES:
                         transpose_bunch(phase + 2)
+                    if phase == 0:
+                        spread_bias(1)
                     if closed is not None:
                         add_partitions(closed[0], closed[1])
                         closed = None

@@ -34,8 +34,9 @@ N_UNITS = N_GROUPS * RUN // UNIT
 UNITS_PER_GROUP = RUN // UNIT
 N_PHASES = 2 * N_UNITS
 SCALAR_EVERY = 4
-GPSIMD_SLOT = 2
-N_PSUM_SLOTS = RUN - UNITS_PER_GROUP
+GPSIMD_ADDS = ((1, 2), (10,))
+GPSIMD_SLOTS = (1, 2, 10)
+N_PSUM_SLOTS = RUN - len(GPSIMD_SLOTS)
 TAIL_SLOTS = 2
 
 FLOPS = 2 * TOKENS * WIDTH * 2 * WIDTH
@@ -74,7 +75,7 @@ def tile_chunkedattention_pb_t_kernel(
         ones = const.tile([P, P], BF16)
         ident = const.tile([P, P], F32)
         bias = const.tile([P, 2, WIDTH], F32)
-        bias_psum_slots = const.tile([P, 2, WIDTH], F32)
+        bias_t = const.tile([P, 2, HEADS, N_CHUNKS], F32)
         means_t = const.tile([P, 2, HEADS, N_CHUNKS], F32)
         mean_rows = const.tile([P, 2 * MEAN_ROWS // P, HEAD_DIM], F32)
 
@@ -123,7 +124,17 @@ def tile_chunkedattention_pb_t_kernel(
                 out=spread[:], lhsT=ones[:], rhs=bias_row[:, kv * WIDTH : (kv + 1) * WIDTH], start=True, stop=True
             )
             nc.vector.tensor_copy(out=bias[:, kv, :], in_=spread[:])
-            nc.vector.tensor_scalar_mul(out=bias_psum_slots[:, kv, :], in0=bias[:, kv, :], scalar1=float(N_PSUM_SLOTS))
+
+        def spread_missing_biases():
+            turned = psum_prod.tile([P, 2, HEADS, N_CHUNKS], F32, tag="prod")
+            for kv in range(2):
+                for h in range(HEADS):
+                    first = kv * WIDTH + h * HEAD_DIM
+                    nc.tensor.matmul(
+                        out=turned[:, kv, h, :], lhsT=bias_row[:, first : first + HEAD_DIM], rhs=ones[:, 0:N_CHUNKS],
+                        start=True, stop=True,
+                    )
+            nc.scalar.mul(out=bias_t[:], in_=turned[:], mul=float(N_PSUM_SLOTS * PARTS_PER_CHUNK))
 
         def sort_bunch(b):
             x_sorted = sorted_pool.tile([P, BUNCH, 2, P], F32)
@@ -185,11 +196,15 @@ def tile_chunkedattention_pb_t_kernel(
                 nc.tensor.transpose(
                     flipped[:, h, :], sums_tiles[(g, kv)][:, h * HEAD_DIM : (h + 1) * HEAD_DIM], ident[:]
                 )
+            chunks = slice(g * CHUNKS_PER_GROUP, (g + 1) * CHUNKS_PER_GROUP)
             nc.vector.tensor_reduce(
-                out=means_t[:, kv, :, g * CHUNKS_PER_GROUP : (g + 1) * CHUNKS_PER_GROUP],
+                out=means_t[:, kv, :, chunks],
                 in_=flipped[:].rearrange("d h (c i) -> d h c i", i=PARTS_PER_CHUNK),
                 axis=mybir.AxisListType.X,
                 op=ADD,
+            )
+            nc.vector.tensor_tensor(
+                out=means_t[:, kv, :, chunks], in0=means_t[:, kv, :, chunks], in1=bias_t[:, kv, :, chunks], op=ADD
             )
 
         transpose_bunch(0, direct=True)
@@ -218,10 +233,11 @@ def tile_chunkedattention_pb_t_kernel(
                         transpose_bunch(phase + 2)
                     if phase == 0:
                         spread_bias(1)
+                        spread_missing_biases()
                     if closed is not None:
                         add_partitions(closed[0], closed[1])
                         closed = None
-                if i != GPSIMD_SLOT:
+                if in_group not in GPSIMD_SLOTS:
                     project(acc_tiles[kv], slot, kv, start=(in_group == 0), stop=(in_group == RUN - 1))
                 prod = psum_prod.tile([P, WIDTH], F32, tag="prod")
                 project(prod, slot, kv, start=True, stop=True)
@@ -231,14 +247,15 @@ def tile_chunkedattention_pb_t_kernel(
                     nc.gpsimd.tensor_tensor(out=rows[:, :, i, :], in0=rows[:, :, i, :], in1=bias_kv, op=ADD)
                 else:
                     nc.vector.tensor_tensor(out=rows[:, :, i, :], in0=prod_heads, in1=bias_kv, op=ADD)
-                if i == GPSIMD_SLOT:
-                    if unit_in_group == 0:
-                        extra = extra_pool.tile([P, HEADS, HEAD_DIM], F32, tag="extra%d" % kv)
-                        extra_tiles[kv] = extra
-                        so_far = bias_psum_slots[:, kv, :].rearrange("p (h d) -> p h d", h=HEADS)
-                    else:
-                        so_far = extra_tiles[kv][:]
-                    nc.gpsimd.tensor_tensor(out=extra_tiles[kv][:], in0=rows[:, :, i, :], in1=so_far, op=ADD)
+                for slots in GPSIMD_ADDS:
+                    if in_group == slots[-1]:
+                        if len(slots) == 2:
+                            extra = extra_pool.tile([P, HEADS, HEAD_DIM], F32, tag="extra%d" % kv)
+                            extra_tiles[kv] = extra
+                            so_far = rows[:, :, slots[0] % UNIT, :]
+                        else:
+                            so_far = extra_tiles[kv][:]
+                        nc.gpsimd.tensor_tensor(out=extra_tiles[kv][:], in0=rows[:, :, i, :], in1=so_far, op=ADD)
                 if i == 0 and phase + 3 < N_BUNCHES:
                     sort_bunch(phase + 3)
                 if (i + 1) % store_slots == 0:

@@ -11,6 +11,7 @@ U8 = mybir.dt.uint8
 FP8X4 = mybir.dt.float8_e4m3fn_x4
 FP4X4 = mybir.dt.float4_e2m1fn_x4
 ADD = mybir.AluOpType.add
+MULT = mybir.AluOpType.mult
 
 P = 128
 TOKENS = 6144
@@ -76,6 +77,7 @@ def tile_chunkedattention_pb_t_kernel(
         ident = const.tile([P, P], F32)
         bias = const.tile([P, 2, WIDTH], F32)
         bias_t = const.tile([P, 2, HEADS, N_CHUNKS], F32)
+        bias_rows = const.tile([P, 2 * MEAN_ROWS // P, HEAD_DIM], F32)
         means_t = const.tile([P, 2, HEADS, N_CHUNKS], F32)
         mean_rows = const.tile([P, 2 * MEAN_ROWS // P, HEAD_DIM], F32)
 
@@ -125,7 +127,7 @@ def tile_chunkedattention_pb_t_kernel(
             )
             nc.vector.tensor_copy(out=bias[:, kv, :], in_=spread[:])
 
-        def spread_missing_biases():
+        def turn_biases():
             turned = psum_prod.tile([P, 2, HEADS, N_CHUNKS], F32, tag="prod")
             for kv in range(2):
                 for h in range(HEADS):
@@ -134,7 +136,14 @@ def tile_chunkedattention_pb_t_kernel(
                         out=turned[:, kv, h, :], lhsT=bias_row[:, first : first + HEAD_DIM], rhs=ones[:, 0:N_CHUNKS],
                         start=True, stop=True,
                     )
-            nc.scalar.mul(out=bias_t[:], in_=turned[:], mul=float(N_PSUM_SLOTS * PARTS_PER_CHUNK))
+            nc.scalar.copy(out=bias_t[:], in_=turned[:])
+
+        def spread_missing_biases():
+            cols = bias_t[:].rearrange("d a h c -> d (a h c)")
+            back = psum_prod.tile([P, 2 * MEAN_ROWS // P, HEAD_DIM], F32, tag="prod")
+            for r in range(2 * MEAN_ROWS // P):
+                nc.tensor.transpose(back[:, r, :], cols[:, r * P : (r + 1) * P], ident[:])
+            nc.scalar.mul(out=bias_rows[:], in_=back[:], mul=float(N_PSUM_SLOTS) / RUN)
 
         def sort_bunch(b):
             x_sorted = sorted_pool.tile([P, BUNCH, 2, P], F32)
@@ -203,9 +212,6 @@ def tile_chunkedattention_pb_t_kernel(
                 axis=mybir.AxisListType.X,
                 op=ADD,
             )
-            nc.vector.tensor_tensor(
-                out=means_t[:, kv, :, chunks], in0=means_t[:, kv, :, chunks], in1=bias_t[:, kv, :, chunks], op=ADD
-            )
 
         transpose_bunch(0, direct=True)
         quantise_bunch(0, pieces=2)
@@ -233,6 +239,8 @@ def tile_chunkedattention_pb_t_kernel(
                         transpose_bunch(phase + 2)
                     if phase == 0:
                         spread_bias(1)
+                        turn_biases()
+                    if phase == 1:
                         spread_missing_biases()
                     if closed is not None:
                         add_partitions(closed[0], closed[1])
@@ -276,7 +284,9 @@ def tile_chunkedattention_pb_t_kernel(
         flipped_back = psum_prod.tile([P, n_blocks, HEAD_DIM], F32, tag="prod")
         for r in range(n_blocks):
             nc.tensor.transpose(flipped_back[:, r, :], means_t_cols[:, r * P : (r + 1) * P], ident[:])
-        nc.scalar.mul(out=mean_rows[:], in_=flipped_back[:], mul=1.0 / CHUNK)
+        nc.vector.scalar_tensor_tensor(
+            out=mean_rows[:], in0=flipped_back[:], scalar=1.0 / CHUNK, in1=bias_rows[:], op0=MULT, op1=ADD
+        )
         for kv in range(2):
             for r in range(n_blocks):
                 low = max(kv * MEAN_ROWS, r * P)

@@ -38,7 +38,6 @@ SCALAR_EVERY = 4
 GPSIMD_ADDS = ((1, 2), (10,))
 GPSIMD_SLOTS = (1, 2, 10)
 N_PSUM_SLOTS = RUN - len(GPSIMD_SLOTS)
-TAIL_SLOTS = 2
 
 FLOPS = 2 * TOKENS * WIDTH * 2 * WIDTH
 
@@ -224,7 +223,6 @@ def tile_chunkedattention_pb_t_kernel(
             unit, kv = divmod(phase, 2)
             g, unit_in_group = divmod(unit, UNITS_PER_GROUP)
             bias_kv = bias[:, kv, :].rearrange("p (h d) -> p h d", h=HEADS)
-            store_slots = TAIL_SLOTS if phase == N_PHASES - 1 else UNIT
             if phase + 1 < N_BUNCHES:
                 quantise_bunch(phase + 1)
             if unit_in_group == 0:
@@ -266,10 +264,8 @@ def tile_chunkedattention_pb_t_kernel(
                         nc.gpsimd.tensor_tensor(out=extra_tiles[kv][:], in0=rows[:, :, i, :], in1=so_far, op=ADD)
                 if i == 0 and phase + 3 < N_BUNCHES:
                     sort_bunch(phase + 3)
-                if (i + 1) % store_slots == 0:
-                    done = slice(i + 1 - store_slots, i + 1)
-                    in_run = slice(in_group + 1 - store_slots, in_group + 1)
-                    nc.sync.dma_start(out=rows_out[kv][g, :, :, in_run, :], in_=rows[:, :, done, :])
+            in_run = slice(unit_in_group * UNIT, (unit_in_group + 1) * UNIT)
+            nc.sync.dma_start(out=rows_out[kv][g, :, :, in_run, :], in_=rows[:])
             if unit_in_group == UNITS_PER_GROUP - 1:
                 sums = sums_pool.tile([P, WIDTH], F32)
                 nc.vector.tensor_tensor(

@@ -288,7 +288,7 @@ def tile_chunkedattention_pb_t_kernel(
                 low = max(kv * MEAN_ROWS, r * P)
                 high = min((kv + 1) * MEAN_ROWS, (r + 1) * P)
                 if low < high:
-                    nc.sync.dma_start(
+                    nc.scalar.dma_start(
                         out=means_out[kv][low - kv * MEAN_ROWS : high - kv * MEAN_ROWS, :],
                         in_=mean_rows[low - r * P : high - r * P, r, :],
                     )

@@ -49,7 +49,7 @@ def tile_chunkedattention_pb_t_kernel(
     with ExitStack() as ctx:
         ctx.enter_context(tc.manual_schedule())
         const = ctx.enter_context(tc.tile_pool(name="const", bufs=1))
-        x_pool = ctx.enter_context(tc.tile_pool(name="x", bufs=N_BUNCHES))
+        x_pool = ctx.enter_context(tc.tile_pool(name="x", bufs=1))
         sorted_pool = ctx.enter_context(tc.tile_pool(name="sorted", bufs=3))
         grouped_pool = ctx.enter_context(tc.tile_pool(name="grouped", bufs=3))
         codes_pool = ctx.enter_context(tc.tile_pool(name="codes", bufs=4))
@@ -85,11 +85,15 @@ def tile_chunkedattention_pb_t_kernel(
         nc.vector.memset(ones[:], 1.0)
         make_identity(nc, ident[:])
 
-        def load_x(b):
-            x_b = x_pool.tile([P, BUNCH, WIDTH], BF16)
+        x_tiles = []
+
+        def load_x(bunches):
+            b = len(x_tiles)
+            x_b = x_pool.tile([P, bunches * BUNCH, WIDTH], BF16, tag="x%d" % b)
             g, first = divmod(b * BUNCH, RUN)
-            nc.sync.dma_start(out=x_b[:], in_=x_rows[g, :, first : first + BUNCH, :])
-            return x_b
+            nc.sync.dma_start(out=x_b[:], in_=x_rows[g, :, first : first + bunches * BUNCH, :])
+            for s in range(0, bunches * BUNCH, BUNCH):
+                x_tiles.append(x_b[:, s : s + BUNCH, :])
 
         def load_weight(kv):
             nc.sync.dma_start(out=w_words[:, kv, :].bitcast(I32), in_=words_in[kv][0].bitcast(I32))
@@ -100,17 +104,17 @@ def tile_chunkedattention_pb_t_kernel(
                 )
 
         def load_bias(kv):
-            nc.sync.dma_start(out=bias_row[0:1, kv * WIDTH : (kv + 1) * WIDTH], in_=bias_in[kv].unsqueeze(0))
+            nc.gpsimd.dma_start(out=bias_row[0:1, kv * WIDTH : (kv + 1) * WIDTH], in_=bias_in[kv].unsqueeze(0))
 
-        x_tiles = [load_x(0)]
+        for kv in range(2):
+            load_bias(kv)
+        load_x(1)
         load_weight(0)
-        x_tiles.append(load_x(1))
-        load_bias(0)
-        x_tiles.append(load_x(2))
-        load_bias(1)
+        for b in range(3):
+            load_x(1)
         load_weight(1)
-        for b in range(3, N_BUNCHES):
-            x_tiles.append(load_x(b))
+        for b in range(4):
+            load_x(2)
 
         sorted_tiles = {}
         grouped_tiles = {}

@@ -69,8 +69,8 @@ def tile_chunkedattention_pb_t_kernel(
         ]
         means_out = [o[0].rearrange("h c d -> (h c) d") for o in (out_2, out_3)]
 
-        w_words = const.tile([P, 2, 2 * WIDTH], U8, align_bytes=64)
-        w_scales = const.tile([P, 2, WIDTH], U8, align_bytes=64)
+        w_words = const.tile([P, 2, 2 * WIDTH], U8, align_bytes=256)
+        w_scales = const.tile([P, 2, WIDTH], U8, align_bytes=256)
         bias_row = const.tile([P, 2 * WIDTH], BF16)
         ones = const.tile([P, P], BF16)
         ident = const.tile([P, P], F32)
@@ -177,8 +177,8 @@ def tile_chunkedattention_pb_t_kernel(
             grouped_tiles[b] = grouped
 
         def quantise_bunch(b, pieces=1):
-            codes = codes_pool.tile([P, BUNCH * P], U32, align_bytes=64)
-            planes = codes_pool.tile([P, BUNCH * P], U8, align_bytes=64)
+            codes = codes_pool.tile([P, BUNCH * P], U32, align_bytes=256)
+            planes = codes_pool.tile([P, BUNCH * P], U8, align_bytes=256)
             n = BUNCH // pieces
             for s in range(0, BUNCH, n):
                 cols = slice(s * P, (s + n) * P)

@@ -34,10 +34,31 @@ N_BUNCHES = N_GROUPS * RUN // BUNCH
 N_UNITS = N_GROUPS * RUN // UNIT
 UNITS_PER_GROUP = RUN // UNIT
 N_PHASES = 2 * N_UNITS
-SCALAR_EVERY = 4
 GPSIMD_ADDS = ((1, 2), (10,))
-GPSIMD_SLOTS = (1, 2, 10)
+GPSIMD_SLOTS = tuple(j for s in GPSIMD_ADDS for j in s)
 N_PSUM_SLOTS = RUN - len(GPSIMD_SLOTS)
+
+QUANT_AT = 1
+QUANT_PIECES = 1
+TURN_AT = 4
+ADD_AT = 4
+ADD_PHASES = ()
+ADD_MOST = 1
+LAST_STORES = ()
+V_REVERSED = False
+PROD_FIRST = True
+BIAS_STEP = 4
+T1_BANK = 0
+T2_BANK = 4
+Q1_BANK = 1
+SORT2_BANK = 0
+N_DIRECT = 2
+FIRST_PIECES = 1
+VECTOR_COPIES = ((1, 1),)
+FIRST_SCALAR = (0, 4)
+JOIN_AT = 0
+SORT_AT = 0
+SCALAR_SLOTS = ((0, 4),)
 
 FLOPS = 2 * TOKENS * WIDTH * 2 * WIDTH
 
@@ -52,9 +73,9 @@ def tile_chunkedattention_pb_t_kernel(
         x_pool = ctx.enter_context(tc.tile_pool(name="x", bufs=1))
         sorted_pool = ctx.enter_context(tc.tile_pool(name="sorted", bufs=3))
         grouped_pool = ctx.enter_context(tc.tile_pool(name="grouped", bufs=3))
-        codes_pool = ctx.enter_context(tc.tile_pool(name="codes", bufs=4))
+        codes_pool = ctx.enter_context(tc.tile_pool(name="codes", bufs=6))
         out_pool = ctx.enter_context(tc.tile_pool(name="out", bufs=5))
-        sums_pool = ctx.enter_context(tc.tile_pool(name="sums", bufs=2))
+        sums_pool = ctx.enter_context(tc.tile_pool(name="sums", bufs=6))
         extra_pool = ctx.enter_context(tc.tile_pool(name="extra", bufs=2))
         psum_prod = ctx.enter_context(tc.psum_pool(name="psum_prod", bufs=6))
         psum_acc = ctx.enter_context(tc.psum_pool(name="psum_acc", bufs=1))
@@ -87,11 +108,13 @@ def tile_chunkedattention_pb_t_kernel(
 
         x_tiles = []
 
-        def load_x(bunches):
+        def load_x(bunches, pieces=1):
             b = len(x_tiles)
             x_b = x_pool.tile([P, bunches * BUNCH, WIDTH], BF16, tag="x%d" % b)
             g, first = divmod(b * BUNCH, RUN)
-            nc.sync.dma_start(out=x_b[:], in_=x_rows[g, :, first : first + bunches * BUNCH, :])
+            n = bunches * BUNCH // pieces
+            for s in range(0, bunches * BUNCH, n):
+                nc.sync.dma_start(out=x_b[:, s : s + n, :], in_=x_rows[g, :, first + s : first + s + n, :])
             for s in range(0, bunches * BUNCH, BUNCH):
                 x_tiles.append(x_b[:, s : s + BUNCH, :])
 
@@ -108,7 +131,7 @@ def tile_chunkedattention_pb_t_kernel(
 
         for kv in range(2):
             load_bias(kv)
-        load_x(1)
+        load_x(1, pieces=FIRST_PIECES)
         load_weight(0)
         for b in range(3):
             load_x(1)
@@ -159,7 +182,7 @@ def tile_chunkedattention_pb_t_kernel(
             sorted_tiles[b] = x_sorted
 
         def transpose_bunch(b, direct=False):
-            grouped = grouped_pool.tile([P, BUNCH, P, 4], BF16, align_bytes=64)
+            grouped = grouped_pool.tile([P, BUNCH, P, 4], BF16, align_bytes=256)
             grouped_words = grouped[:].bitcast(F32)
             for pair in range(BUNCH // 2):
                 xt = psum_prod.tile([P, 2, 2, P], F32, tag="prod")
@@ -170,10 +193,12 @@ def tile_chunkedattention_pb_t_kernel(
                             nc.tensor.transpose(xt[:, s, u, :], words[:, u : WIDTH // 2 : 2], ident[:])
                         else:
                             nc.tensor.transpose(xt[:, s, u, :], sorted_tiles[b][:, 2 * pair + s, u, :], ident[:])
-                nc.scalar.copy(
-                    out=grouped_words[:, 2 * pair : 2 * pair + 2, :, :],
-                    in_=xt[:].rearrange("p s u t -> p s t u"),
-                )
+                out = grouped_words[:, 2 * pair : 2 * pair + 2, :, :]
+                words_t = xt[:].rearrange("p s u t -> p s t u")
+                if (b, pair) in VECTOR_COPIES:
+                    nc.vector.tensor_copy(out=out, in_=words_t)
+                else:
+                    nc.scalar.copy(out=out, in_=words_t)
             grouped_tiles[b] = grouped
 
         def quantise_bunch(b, pieces=1):
@@ -216,69 +241,94 @@ def tile_chunkedattention_pb_t_kernel(
                 op=ADD,
             )
 
+        def join_sums(g, kv):
+            sums = sums_pool.tile([P, WIDTH], F32)
+            nc.vector.tensor_tensor(
+                out=sums[:], in0=acc_tiles[kv][:], in1=extra_tiles[kv][:].rearrange("p h d -> p (h d)"), op=ADD
+            )
+            sums_tiles[(g, kv)] = sums
+
         transpose_bunch(0, direct=True)
         quantise_bunch(0, pieces=2)
-        transpose_bunch(1, direct=True)
         spread_bias(0)
-        sort_bunch(2)
 
-        closed = None
+        to_join = None
+        closed = []
         for phase in range(N_PHASES):
             unit, kv = divmod(phase, 2)
             g, unit_in_group = divmod(unit, UNITS_PER_GROUP)
             bias_kv = bias[:, kv, :].rearrange("p (h d) -> p h d", h=HEADS)
-            if phase + 1 < N_BUNCHES:
-                quantise_bunch(phase + 1)
             if unit_in_group == 0:
                 acc = psum_acc.tile([P, WIDTH], F32, tag="acc%d" % kv)
                 acc_tiles[kv] = acc
             rows = out_pool.tile([P, HEADS, UNIT, HEAD_DIM], F32)
-            for i in range(UNIT):
+            stored = 0
+            for step in range(UNIT):
+                i = UNIT - 1 - step if kv == 1 and V_REVERSED else step
                 slot = unit * UNIT + i
                 in_group = slot % RUN
-                if i == UNIT // 2:
+                bank = phase * UNIT + step
+                if bank == T1_BANK:
+                    transpose_bunch(1, direct=True)
+                if bank == SORT2_BANK and N_DIRECT < 3:
+                    sort_bunch(2)
+                if (step == QUANT_AT and phase > 0 or bank == Q1_BANK) and phase + 1 < N_BUNCHES:
+                    quantise_bunch(phase + 1, pieces=QUANT_PIECES)
+                if step == TURN_AT and phase > 0 or bank == T2_BANK:
                     if phase + 2 < N_BUNCHES:
-                        transpose_bunch(phase + 2)
+                        transpose_bunch(phase + 2, direct=phase + 2 < N_DIRECT)
+                if step == BIAS_STEP:
                     if phase == 0:
                         spread_bias(1)
                         turn_biases()
                     if phase == 1:
                         spread_missing_biases()
-                    if closed is not None:
-                        add_partitions(closed[0], closed[1])
-                        closed = None
-                if in_group not in GPSIMD_SLOTS:
-                    project(acc_tiles[kv], slot, kv, start=(in_group == 0), stop=(in_group == RUN - 1))
+                if step == ADD_AT and phase in ADD_PHASES:
+                    for done in closed[:ADD_MOST]:
+                        add_partitions(done[0], done[1])
+                    closed = closed[ADD_MOST:]
+                if step == JOIN_AT and to_join is not None:
+                    join_sums(to_join[0], to_join[1])
+                    closed.append(to_join)
+                    to_join = None
+                order = [(s, UNIT - 1 - s if kv == 1 and V_REVERSED else s) for s in range(UNIT)]
+                order = [u * UNIT + s for u in range(UNITS_PER_GROUP) for s in [q[1] for q in order]]
+                order = [s for s in order if s not in GPSIMD_SLOTS]
+                if in_group in order and not PROD_FIRST:
+                    project(acc_tiles[kv], slot, kv, start=(in_group == order[0]), stop=(in_group == order[-1]))
                 prod = psum_prod.tile([P, WIDTH], F32, tag="prod")
                 project(prod, slot, kv, start=True, stop=True)
+                if in_group in order and PROD_FIRST:
+                    project(acc_tiles[kv], slot, kv, start=(in_group == order[0]), stop=(in_group == order[-1]))
                 prod_heads = prod[:].rearrange("p (h d) -> p h d", h=HEADS)
-                if i % SCALAR_EVERY == 0:
+                if step in (SCALAR_SLOTS[phase % len(SCALAR_SLOTS)] if phase > 0 else FIRST_SCALAR):
                     nc.scalar.copy(out=rows[:, :, i, :], in_=prod_heads)
                     nc.gpsimd.tensor_tensor(out=rows[:, :, i, :], in0=rows[:, :, i, :], in1=bias_kv, op=ADD)
                 else:
                     nc.vector.tensor_tensor(out=rows[:, :, i, :], in0=prod_heads, in1=bias_kv, op=ADD)
                 for slots in GPSIMD_ADDS:
-                    if in_group == slots[-1]:
+                    if in_group == (slots[0] if kv == 1 and V_REVERSED else slots[-1]):
                         if len(slots) == 2:
                             extra = extra_pool.tile([P, HEADS, HEAD_DIM], F32, tag="extra%d" % kv)
                             extra_tiles[kv] = extra
-                            so_far = rows[:, :, slots[0] % UNIT, :]
+                            so_far = rows[:, :, (slots[1] if kv == 1 and V_REVERSED else slots[0]) % UNIT, :]
                         else:
                             so_far = extra_tiles[kv][:]
                         nc.gpsimd.tensor_tensor(out=extra_tiles[kv][:], in0=rows[:, :, i, :], in1=so_far, op=ADD)
-                if i == 0 and phase + 3 < N_BUNCHES:
+                if step == SORT_AT and phase + 3 < N_BUNCHES and phase + 3 >= N_DIRECT:
                     sort_bunch(phase + 3)
-            in_run = slice(unit_in_group * UNIT, (unit_in_group + 1) * UNIT)
-            nc.sync.dma_start(out=rows_out[kv][g, :, :, in_run, :], in_=rows[:])
+                if step == UNIT - 1 or phase == N_PHASES - 1 and step in LAST_STORES:
+                    low, high = (i, UNIT - stored) if kv == 1 and V_REVERSED else (stored, i + 1)
+                    in_run = slice(unit_in_group * UNIT + low, unit_in_group * UNIT + high)
+                    nc.sync.dma_start(out=rows_out[kv][g, :, :, in_run, :], in_=rows[:, :, low:high, :])
+                    stored = step + 1
             if unit_in_group == UNITS_PER_GROUP - 1:
-                sums = sums_pool.tile([P, WIDTH], F32)
-                nc.vector.tensor_tensor(
-                    out=sums[:], in0=acc_tiles[kv][:], in1=extra_tiles[kv][:].rearrange("p h d -> p (h d)"), op=ADD
-                )
-                sums_tiles[(g, kv)] = sums
-                closed = (g, kv)
+                to_join = (g, kv)
 
-        add_partitions(closed[0], closed[1])
+        join_sums(to_join[0], to_join[1])
+        closed.append(to_join)
+        for done in closed:
+            add_partitions(done[0], done[1])
         means_t_cols = means_t[:].rearrange("d a h c -> d (a h c)")
         n_blocks = 2 * MEAN_ROWS // P
         flipped_back = psum_prod.tile([P, n_blocks, HEAD_DIM], F32, tag="prod")

@@ -34,7 +34,7 @@ N_BUNCHES = N_GROUPS * RUN // BUNCH
 N_UNITS = N_GROUPS * RUN // UNIT
 UNITS_PER_GROUP = RUN // UNIT
 N_PHASES = 2 * N_UNITS
-GPSIMD_ADDS = ((1, 2), (10,))
+GPSIMD_ADDS = ((1, 2), (4,), (10,))
 GPSIMD_SLOTS = tuple(j for s in GPSIMD_ADDS for j in s)
 N_PSUM_SLOTS = RUN - len(GPSIMD_SLOTS)
 
@@ -55,10 +55,10 @@ SORT2_BANK = 0
 N_DIRECT = 2
 FIRST_PIECES = 1
 VECTOR_COPIES = ((1, 1),)
-FIRST_SCALAR = (0, 4)
+FIRST_SCALAR = (0,)
 JOIN_AT = 0
 SORT_AT = 0
-SCALAR_SLOTS = ((0, 4),)
+SCALAR_SLOTS = ((0,), (0,), (0, 4), (0, 4))
 
 FLOPS = 2 * TOKENS * WIDTH * 2 * WIDTH
 

@@ -48,12 +48,16 @@ LAST_STORES = ()
 V_REVERSED = False
 PROD_FIRST = True
 BIAS_STEP = 4
+STORE_STEP = None
+LOADS_BEFORE = (1, 1, 1)
+LOADS_AFTER = (4, 4)
+STORE_KV = 1
 T1_BANK = 0
 T2_BANK = 4
 Q1_BANK = 1
 SORT2_BANK = 0
 N_DIRECT = 2
-FIRST_PIECES = 1
+FIRST_PIECES = 2
 VECTOR_COPIES = ((1, 1),)
 FIRST_SCALAR = (0,)
 JOIN_AT = 0
@@ -133,11 +137,11 @@ def tile_chunkedattention_pb_t_kernel(
             load_bias(kv)
         load_x(1, pieces=FIRST_PIECES)
         load_weight(0)
-        for b in range(3):
-            load_x(1)
+        for bunches in LOADS_BEFORE:
+            load_x(bunches)
         load_weight(1)
-        for b in range(4):
-            load_x(2)
+        for bunches in LOADS_AFTER:
+            load_x(bunches)
 
         sorted_tiles = {}
         grouped_tiles = {}
@@ -253,6 +257,7 @@ def tile_chunkedattention_pb_t_kernel(
         spread_bias(0)
 
         to_join = None
+        late_store = None
         closed = []
         for phase in range(N_PHASES):
             unit, kv = divmod(phase, 2)
@@ -315,12 +320,19 @@ def tile_chunkedattention_pb_t_kernel(
                         else:
                             so_far = extra_tiles[kv][:]
                         nc.gpsimd.tensor_tensor(out=extra_tiles[kv][:], in0=rows[:, :, i, :], in1=so_far, op=ADD)
+                if late_store is not None and step == STORE_STEP:
+                    nc.scalar.dma_start(out=late_store[0], in_=late_store[1])
+                    late_store = None
                 if step == SORT_AT and phase + 3 < N_BUNCHES and phase + 3 >= N_DIRECT:
                     sort_bunch(phase + 3)
                 if step == UNIT - 1 or phase == N_PHASES - 1 and step in LAST_STORES:
                     low, high = (i, UNIT - stored) if kv == 1 and V_REVERSED else (stored, i + 1)
                     in_run = slice(unit_in_group * UNIT + low, unit_in_group * UNIT + high)
-                    nc.sync.dma_start(out=rows_out[kv][g, :, :, in_run, :], in_=rows[:, :, low:high, :])
+                    store = (rows_out[kv][g, :, :, in_run, :], rows[:, :, low:high, :])
+                    if kv == STORE_KV and phase < N_PHASES - 1 and STORE_STEP is not None:
+                        late_store = store
+                    else:
+                        nc.sync.dma_start(out=store[0], in_=store[1])
                     stored = step + 1
             if unit_in_group == UNITS_PER_GROUP - 1:
                 to_join = (g, kv)

from contextlib import ExitStack

import concourse.mybir as mybir
from concourse.masks import make_identity

F32 = mybir.dt.float32
BF16 = mybir.dt.bfloat16
I32 = mybir.dt.int32
U32 = mybir.dt.uint32
U8 = mybir.dt.uint8
FP8X4 = mybir.dt.float8_e4m3fn_x4
FP4X4 = mybir.dt.float4_e2m1fn_x4
ADD = mybir.AluOpType.add
MULT = mybir.AluOpType.mult

P = 128
TOKENS = 6144
WIDTH = 512
HEADS = 4
HEAD_DIM = 128
CHUNK = 128
N_CHUNKS = TOKENS // CHUNK
MEAN_ROWS = HEADS * N_CHUNKS

RUN = 16
GROUP = P * RUN
N_GROUPS = TOKENS // GROUP
PARTS_PER_CHUNK = CHUNK // RUN
CHUNKS_PER_GROUP = GROUP // CHUNK

BUNCH = 4
UNIT = 8
N_BUNCHES = N_GROUPS * RUN // BUNCH
N_UNITS = N_GROUPS * RUN // UNIT
UNITS_PER_GROUP = RUN // UNIT
N_PHASES = 2 * N_UNITS
GPSIMD_ADDS = ((1, 2), (4,), (10,))
GPSIMD_SLOTS = tuple(j for s in GPSIMD_ADDS for j in s)
N_PSUM_SLOTS = RUN - len(GPSIMD_SLOTS)

QUANT_AT = 1
QUANT_PIECES = 1
TURN_AT = 4
ADD_AT = 4
ADD_PHASES = ()
ADD_MOST = 1
LAST_STORES = ()
V_REVERSED = False
PROD_FIRST = True
BIAS_STEP = 4
STORE_STEP = None
LOADS_BEFORE = (1, 1, 1)
LOADS_AFTER = (4, 4)
STORE_KV = 1
T1_BANK = 0
T2_BANK = 4
Q1_BANK = 1
SORT2_BANK = 0
N_DIRECT = 2
FIRST_PIECES = 2
VECTOR_COPIES = ((1, 1),)
FIRST_SCALAR = (0,)
JOIN_AT = 0
SORT_AT = 0
SCALAR_SLOTS = ((0,), (0,), (0, 4), (0, 4))

FLOPS = 2 * TOKENS * WIDTH * 2 * WIDTH


def tile_chunkedattention_pb_t_kernel(
    tc, hidden_states, wk_words, wk_scales, bk, wv_words, wv_scales, bv, out_0, out_1, out_2, out_3
):
    nc = tc.nc
    with ExitStack() as ctx:
        ctx.enter_context(tc.manual_schedule())
        const = ctx.enter_context(tc.tile_pool(name="const", bufs=1))
        x_pool = ctx.enter_context(tc.tile_pool(name="x", bufs=1))
        sorted_pool = ctx.enter_context(tc.tile_pool(name="sorted", bufs=3))
        grouped_pool = ctx.enter_context(tc.tile_pool(name="grouped", bufs=3))
        codes_pool = ctx.enter_context(tc.tile_pool(name="codes", bufs=6))
        out_pool = ctx.enter_context(tc.tile_pool(name="out", bufs=5))
        sums_pool = ctx.enter_context(tc.tile_pool(name="sums", bufs=6))
        extra_pool = ctx.enter_context(tc.tile_pool(name="extra", bufs=2))
        psum_prod = ctx.enter_context(tc.psum_pool(name="psum_prod", bufs=6))
        psum_acc = ctx.enter_context(tc.psum_pool(name="psum_acc", bufs=1))

        x_rows = hidden_states[0].rearrange("(g p j) k -> g p j k", p=P, j=RUN)
        words_in = (wk_words, wv_words)
        scales_in = (wk_scales, wv_scales)
        bias_in = (bk, bv)
        rows_out = [
            o[0].rearrange("h c t d -> h (c t) d").rearrange("h (g p j) d -> g p h j d", p=P, j=RUN)
            for o in (out_0, out_1)
        ]
        means_out = [o[0].rearrange("h c d -> (h c) d") for o in (out_2, out_3)]

        w_words = const.tile([P, 2, 2 * WIDTH], U8, align_bytes=256)
        w_scales = const.tile([P, 2, WIDTH], U8, align_bytes=256)
        bias_row = const.tile([P, 2 * WIDTH], BF16)
        ones = const.tile([P, P], BF16)
        ident = const.tile([P, P], F32)
        bias = const.tile([P, 2, WIDTH], F32)
        bias_t = const.tile([P, 2, HEADS, N_CHUNKS], F32)
        bias_rows = const.tile([P, 2 * MEAN_ROWS // P, HEAD_DIM], F32)
        means_t = const.tile([P, 2, HEADS, N_CHUNKS], F32)
        mean_rows = const.tile([P, 2 * MEAN_ROWS // P, HEAD_DIM], F32)

        nc.vector.memset(bias_row[:].bitcast(I32), 0)
        nc.vector.memset(w_scales[:].bitcast(I32), 0)
        nc.vector.memset(ones[:], 1.0)
        make_identity(nc, ident[:])

        x_tiles = []

        def load_x(bunches, pieces=1):
            b = len(x_tiles)
            x_b = x_pool.tile([P, bunches * BUNCH, WIDTH], BF16, tag="x%d" % b)
            g, first = divmod(b * BUNCH, RUN)
            n = bunches * BUNCH // pieces
            for s in range(0, bunches * BUNCH, n):
                nc.sync.dma_start(out=x_b[:, s : s + n, :], in_=x_rows[g, :, first + s : first + s + n, :])
            for s in range(0, bunches * BUNCH, BUNCH):
                x_tiles.append(x_b[:, s : s + BUNCH, :])

        def load_weight(kv):
            nc.sync.dma_start(out=w_words[:, kv, :].bitcast(I32), in_=words_in[kv][0].bitcast(I32))
            for quad in range(4):
                nc.sync.dma_start(
                    out=w_scales[32 * quad : 32 * quad + 4, kv, :].bitcast(I32),
                    in_=scales_in[kv][0, 4 * quad : 4 * quad + 4, :].bitcast(I32),
                )

        def load_bias(kv):
            nc.gpsimd.dma_start(out=bias_row[0:1, kv * WIDTH : (kv + 1) * WIDTH], in_=bias_in[kv].unsqueeze(0))

        for kv in range(2):
            load_bias(kv)
        load_x(1, pieces=FIRST_PIECES)
        load_weight(0)
        for bunches in LOADS_BEFORE:
            load_x(bunches)
        load_weight(1)
        for bunches in LOADS_AFTER:
            load_x(bunches)

        sorted_tiles = {}
        grouped_tiles = {}
        code_tiles = {}
        acc_tiles = {}
        sums_tiles = {}
        extra_tiles = {}

        def spread_bias(kv):
            spread = psum_prod.tile([P, WIDTH], F32, tag="prod")
            nc.tensor.matmul(
                out=spread[:], lhsT=ones[:], rhs=bias_row[:, kv * WIDTH : (kv + 1) * WIDTH], start=True, stop=True
            )
            nc.vector.tensor_copy(out=bias[:, kv, :], in_=spread[:])

        def turn_biases():
            turned = psum_prod.tile([P, 2, HEADS, N_CHUNKS], F32, tag="prod")
            for kv in range(2):
                for h in range(HEADS):
                    first = kv * WIDTH + h * HEAD_DIM
                    nc.tensor.matmul(
                        out=turned[:, kv, h, :], lhsT=bias_row[:, first : first + HEAD_DIM], rhs=ones[:, 0:N_CHUNKS],
                        start=True, stop=True,
                    )
            nc.scalar.copy(out=bias_t[:], in_=turned[:])

        def spread_missing_biases():
            cols = bias_t[:].rearrange("d a h c -> d (a h c)")
            back = psum_prod.tile([P, 2 * MEAN_ROWS // P, HEAD_DIM], F32, tag="prod")
            for r in range(2 * MEAN_ROWS // P):
                nc.tensor.transpose(back[:, r, :], cols[:, r * P : (r + 1) * P], ident[:])
            nc.scalar.mul(out=bias_rows[:], in_=back[:], mul=float(N_PSUM_SLOTS) / RUN)

        def sort_bunch(b):
            x_sorted = sorted_pool.tile([P, BUNCH, 2, P], F32)
            for pair in range(BUNCH // 2):
                two = slice(2 * pair, 2 * pair + 2)
                nc.scalar.copy(
                    out=x_sorted[:, two, :, :],
                    in_=x_tiles[b][:, two, :].bitcast(F32).rearrange("p s (w u) -> p s u w", u=2),
                )
            sorted_tiles[b] = x_sorted

        def transpose_bunch(b, direct=False):
            grouped = grouped_pool.tile([P, BUNCH, P, 4], BF16, align_bytes=256)
            grouped_words = grouped[:].bitcast(F32)
            for pair in range(BUNCH // 2):
                xt = psum_prod.tile([P, 2, 2, P], F32, tag="prod")
                for s in range(2):
                    for u in range(2):
                        if direct:
                            words = x_tiles[b][:, 2 * pair + s, :].bitcast(F32)
                            nc.tensor.transpose(xt[:, s, u, :], words[:, u : WIDTH // 2 : 2], ident[:])
                        else:
                            nc.tensor.transpose(xt[:, s, u, :], sorted_tiles[b][:, 2 * pair + s, u, :], ident[:])
                out = grouped_words[:, 2 * pair : 2 * pair + 2, :, :]
                words_t = xt[:].rearrange("p s u t -> p s t u")
                if (b, pair) in VECTOR_COPIES:
                    nc.vector.tensor_copy(out=out, in_=words_t)
                else:
                    nc.scalar.copy(out=out, in_=words_t)
            grouped_tiles[b] = grouped

        def quantise_bunch(b, pieces=1):
            codes = codes_pool.tile([P, BUNCH * P], U32, align_bytes=256)
            planes = codes_pool.tile([P, BUNCH * P], U8, align_bytes=256)
            n = BUNCH // pieces
            for s in range(0, BUNCH, n):
                cols = slice(s * P, (s + n) * P)
                nc.vector.quantize_mx(
                    out=codes[:, cols].bitcast(FP8X4),
                    scales=planes[:, cols],
                    in_=grouped_tiles[b][:, s : s + n, :, :].rearrange("p s t f -> p (s t f)"),
                )
            code_tiles[b] = (codes, planes)

        def project(target, slot, kv, start, stop):
            codes, planes = code_tiles[slot // BUNCH]
            cols = slice((slot % BUNCH) * P, (slot % BUNCH + 1) * P)
            nc.tensor.matmul_mx(
                out=target[:],
                lhsT=codes[:, cols].bitcast(FP8X4),
                lhsT_scale=planes[:, cols],
                rhs=w_words[:, kv, :].bitcast(FP4X4),
                rhs_scale=w_scales[:, kv, :],
                start=start,
                stop=stop,
            )

        def add_partitions(g, kv):
            flipped = psum_prod.tile([P, HEADS, P], F32, tag="prod")
            for h in range(HEADS):
                nc.tensor.transpose(
                    flipped[:, h, :], sums_tiles[(g, kv)][:, h * HEAD_DIM : (h + 1) * HEAD_DIM], ident[:]
                )
            chunks = slice(g * CHUNKS_PER_GROUP, (g + 1) * CHUNKS_PER_GROUP)
            nc.vector.tensor_reduce(
                out=means_t[:, kv, :, chunks],
                in_=flipped[:].rearrange("d h (c i) -> d h c i", i=PARTS_PER_CHUNK),
                axis=mybir.AxisListType.X,
                op=ADD,
            )

        def join_sums(g, kv):
            sums = sums_pool.tile([P, WIDTH], F32)
            nc.vector.tensor_tensor(
                out=sums[:], in0=acc_tiles[kv][:], in1=extra_tiles[kv][:].rearrange("p h d -> p (h d)"), op=ADD
            )
            sums_tiles[(g, kv)] = sums

        transpose_bunch(0, direct=True)
        quantise_bunch(0, pieces=2)
        spread_bias(0)

        to_join = None
        late_store = None
        closed = []
        for phase in range(N_PHASES):
            unit, kv = divmod(phase, 2)
            g, unit_in_group = divmod(unit, UNITS_PER_GROUP)
            bias_kv = bias[:, kv, :].rearrange("p (h d) -> p h d", h=HEADS)
            if unit_in_group == 0:
                acc = psum_acc.tile([P, WIDTH], F32, tag="acc%d" % kv)
                acc_tiles[kv] = acc
            rows = out_pool.tile([P, HEADS, UNIT, HEAD_DIM], F32)
            stored = 0
            for step in range(UNIT):
                i = UNIT - 1 - step if kv == 1 and V_REVERSED else step
                slot = unit * UNIT + i
                in_group = slot % RUN
                bank = phase * UNIT + step
                if bank == T1_BANK:
                    transpose_bunch(1, direct=True)
                if bank == SORT2_BANK and N_DIRECT < 3:
                    sort_bunch(2)
                if (step == QUANT_AT and phase > 0 or bank == Q1_BANK) and phase + 1 < N_BUNCHES:
                    quantise_bunch(phase + 1, pieces=QUANT_PIECES)
                if step == TURN_AT and phase > 0 or bank == T2_BANK:
                    if phase + 2 < N_BUNCHES:
                        transpose_bunch(phase + 2, direct=phase + 2 < N_DIRECT)
                if step == BIAS_STEP:
                    if phase == 0:
                        spread_bias(1)
                        turn_biases()
                    if phase == 1:
                        spread_missing_biases()
                if step == ADD_AT and phase in ADD_PHASES:
                    for done in closed[:ADD_MOST]:
                        add_partitions(done[0], done[1])
                    closed = closed[ADD_MOST:]
                if step == JOIN_AT and to_join is not None:
                    join_sums(to_join[0], to_join[1])
                    closed.append(to_join)
                    to_join = None
                order = [(s, UNIT - 1 - s if kv == 1 and V_REVERSED else s) for s in range(UNIT)]
                order = [u * UNIT + s for u in range(UNITS_PER_GROUP) for s in [q[1] for q in order]]
                order = [s for s in order if s not in GPSIMD_SLOTS]
                if in_group in order and not PROD_FIRST:
                    project(acc_tiles[kv], slot, kv, start=(in_group == order[0]), stop=(in_group == order[-1]))
                prod = psum_prod.tile([P, WIDTH], F32, tag="prod")
                project(prod, slot, kv, start=True, stop=True)
                if in_group in order and PROD_FIRST:
                    project(acc_tiles[kv], slot, kv, start=(in_group == order[0]), stop=(in_group == order[-1]))
                prod_heads = prod[:].rearrange("p (h d) -> p h d", h=HEADS)
                if step in (SCALAR_SLOTS[phase % len(SCALAR_SLOTS)] if phase > 0 else FIRST_SCALAR):
                    nc.scalar.copy(out=rows[:, :, i, :], in_=prod_heads)
                    nc.gpsimd.tensor_tensor(out=rows[:, :, i, :], in0=rows[:, :, i, :], in1=bias_kv, op=ADD)
                else:
                    nc.vector.tensor_tensor(out=rows[:, :, i, :], in0=prod_heads, in1=bias_kv, op=ADD)
                for slots in GPSIMD_ADDS:
                    if in_group == (slots[0] if kv == 1 and V_REVERSED else slots[-1]):
                        if len(slots) == 2:
                            extra = extra_pool.tile([P, HEADS, HEAD_DIM], F32, tag="extra%d" % kv)
                            extra_tiles[kv] = extra
                            so_far = rows[:, :, (slots[1] if kv == 1 and V_REVERSED else slots[0]) % UNIT, :]
                        else:
                            so_far = extra_tiles[kv][:]
                        nc.gpsimd.tensor_tensor(out=extra_tiles[kv][:], in0=rows[:, :, i, :], in1=so_far, op=ADD)
                if late_store is not None and step == STORE_STEP:
                    nc.scalar.dma_start(out=late_store[0], in_=late_store[1])
                    late_store = None
                if step == SORT_AT and phase + 3 < N_BUNCHES and phase + 3 >= N_DIRECT:
                    sort_bunch(phase + 3)
                if step == UNIT - 1 or phase == N_PHASES - 1 and step in LAST_STORES:
                    low, high = (i, UNIT - stored) if kv == 1 and V_REVERSED else (stored, i + 1)
                    in_run = slice(unit_in_group * UNIT + low, unit_in_group * UNIT + high)
                    store = (rows_out[kv][g, :, :, in_run, :], rows[:, :, low:high, :])
                    if kv == STORE_KV and phase < N_PHASES - 1 and STORE_STEP is not None:
                        late_store = store
                    else:
                        nc.sync.dma_start(out=store[0], in_=store[1])
                    stored = step + 1
            if unit_in_group == UNITS_PER_GROUP - 1:
                to_join = (g, kv)

        join_sums(to_join[0], to_join[1])
        closed.append(to_join)
        for done in closed:
            add_partitions(done[0], done[1])
        means_t_cols = means_t[:].rearrange("d a h c -> d (a h c)")
        n_blocks = 2 * MEAN_ROWS // P
        flipped_back = psum_prod.tile([P, n_blocks, HEAD_DIM], F32, tag="prod")
        for r in range(n_blocks):
            nc.tensor.transpose(flipped_back[:, r, :], means_t_cols[:, r * P : (r + 1) * P], ident[:])
        nc.vector.scalar_tensor_tensor(
            out=mean_rows[:], in0=flipped_back[:], scalar=1.0 / CHUNK, in1=bias_rows[:], op0=MULT, op1=ADD
        )
        for kv in range(2):
            for r in range(n_blocks):
                low = max(kv * MEAN_ROWS, r * P)
                high = min((kv + 1) * MEAN_ROWS, (r + 1) * P)
                if low < high:
                    nc.scalar.dma_start(
                        out=means_out[kv][low - kv * MEAN_ROWS : high - kv * MEAN_ROWS, :],
                        in_=mean_rows[low - r * P : high - r * P, r, :],
                    )
